import numpy as np
import ml_dtypes


def mxq(x, axis, fmt="e4m3"):
    dtype, down = {"e4m3": (ml_dtypes.float8_e4m3fn, 7), "e5m2": (ml_dtypes.float8_e5m2, 14)}[fmt]
    v = np.moveaxis(np.asarray(x, np.float32).astype(ml_dtypes.bfloat16).astype(np.float64), axis, -1)
    blocks = v.reshape(v.shape[:-1] + (-1, 32))
    amax = np.abs(blocks).max(-1, keepdims=True)
    byte = np.maximum(np.where(amax > 0, np.frexp(amax)[1] - 1 + 127, 0) - down, 1)
    scale = np.exp2(byte - 127.0)
    codes = (blocks / scale).astype(np.float32).astype(dtype).astype(np.float64)
    return np.moveaxis((codes * scale).reshape(v.shape), -1, axis)


WIDE = False


def mx_kscale(k):
    if not WIDE:
        return np.ones(k)
    levels = np.array([10, -10, 5, -5, 0])
    a = np.random.permutation(np.resize(levels, k // 512 * 4)).reshape(k // 512, 4)
    idx = np.arange(k)
    return np.exp2(a[idx // 512, idx % 128 // 32])


BF16 = ml_dtypes.bfloat16


def bf(x):
    return np.asarray(x, np.float32).astype(BF16)


def f64(x):
    return np.asarray(x).astype(np.float64)


B, N, K, D, L = 4, 1024, 7, 512, 256


def setup_inputs():
    s = mx_kscale(D)
    limit = np.sqrt(6.0 / (D + L))
    lone = np.random.random((B, N, 1)) < 0.125
    a = (0.3 + 0.7 * np.random.random((B, N, K + 1))) * np.where(lone, 0.4 / (K + 1), 1.0)
    return {"targets": bf(np.random.standard_normal((B, N, D)) * s),
            "neighbors": bf(np.random.standard_normal((B, N, K, D)) * s),
            "a": bf(a),
            "kernel": bf(np.random.uniform(-limit, limit, (D, L)) / s[:, None])}


def reference(targets, neighbors, a, kernel):
    neighborhood = np.concatenate([f64(targets)[..., None, :], f64(neighbors)], axis=-2)
    y = (mxq(neighborhood, 3, "e4m3") @ mxq(f64(kernel), 0, "e4m3")).sum(axis=-2)
    factor = f64(a).sum(axis=-1, keepdims=True)
    factor = np.where(factor > 0.5, factor, np.ones_like(factor))
    y = y / factor
    return np.maximum(y, 0.0)

@@ -1,0 +1,196 @@
+from contextlib import ExitStack
+
+import concourse.mybir as mybir
+from concourse.masks import make_identity
+
+F32 = mybir.dt.float32
+BF16 = mybir.dt.bfloat16
+U32 = mybir.dt.uint32
+U8 = mybir.dt.uint8
+FP8X4 = mybir.dt.float8_e4m3fn_x4
+ALU = mybir.AluOpType
+ACT = mybir.ActivationFunctionType
+
+P = 128
+NODES = 4096
+TILES = NODES // P
+NBRS = 7
+MEMBERS = NBRS + 1
+D = 512
+L = 256
+WORDS = D // 2
+
+FLOPS = 2 * NODES * MEMBERS * D * L
+
+RUNS = [1, 1] + [2] * 14 + [1, 1]
+NB_CHUNKS = [(0, 1), (1, 1)] + [(j, 2) for j in range(2, 30, 2)] + [(30, 1), (31, 1)]
+TG_CHUNKS = [(0, 1), (1, 3), (4, 4), (8, 8), (16, 8), (24, 8)]
+ST_CHUNKS = [(j, 4) for j in range(0, 28, 4)] + [(28, 2), (30, 1), (31, 1)]
+NB_BUFS = 6
+VECTOR_BANKS = (3,)
+
+
+def tile_singlegcnlayer_t_kernel(tc, targets, neighbors, a, kernel, out):
+    nc = tc.nc
+    tg_v = targets.rearrange("b n d -> (b n) d").rearrange("(p j) d -> p j d", j=TILES)
+    nb_v = neighbors.rearrange("b n k d -> (b n) (k d)").rearrange("(p j) f -> p j f", j=TILES)
+    a_v = a.rearrange("b n k -> (b n) k").rearrange("(p j) k -> p (j k)", j=TILES)
+    out_v = out.rearrange("b n l -> (b n) l").rearrange("(p j) l -> p j l", j=TILES)
+    w_v = kernel.rearrange("(u q e) c -> q u (e c)", u=2, e=2)
+
+    with ExitStack() as ctx:
+        const = ctx.enter_context(tc.tile_pool(name="const", bufs=1))
+        nbp = ctx.enter_context(tc.tile_pool(name="nbp", bufs=NB_BUFS))
+        grp = ctx.enter_context(tc.tile_pool(name="grp", bufs=4))
+        qp = ctx.enter_context(tc.tile_pool(name="qp", bufs=4))
+        stp = ctx.enter_context(tc.tile_pool(name="stp", bufs=3))
+        pst = ctx.enter_context(tc.psum_pool(name="pst", bufs=6))
+        psa = ctx.enter_context(tc.psum_pool(name="psa", bufs=2))
+        ctx.enter_context(tc.manual_schedule())
+
+        ident = const.tile([P, P], F32, name="ident")
+        make_identity(nc, ident[:])
+        warm = const.tile([P, 1], F32, name="warm")
+        nc.scalar.activation(out=warm[:], in_=ident[:, 0:1], func=ACT.Relu)
+
+        src = {}
+        state = {"nb": 0, "tg": 0}
+
+        def load_targets():
+            j0, cnt = TG_CHUNKS[state["tg"]]
+            state["tg"] += 1
+            t = const.tile([P, cnt * D], BF16, name="tg%d" % j0)
+            nc.sync.dma_start(
+                out=t[:].rearrange("p (j d) -> p j d", d=D), in_=tg_v[:, j0 : j0 + cnt, :]
+            )
+            for i in range(cnt):
+                src[(j0 + i, 0)] = (t[:].bitcast(F32), i * WORDS)
+
+        def load_neighbors():
+            j0, cnt = NB_CHUNKS[state["nb"]]
+            state["nb"] += 1
+            while state["tg"] < len(TG_CHUNKS) and TG_CHUNKS[state["tg"]][0] <= j0:
+                load_targets()
+            t = nbp.tile([P, cnt * NBRS * D], BF16, name="nb")
+            nc.sync.dma_start(
+                out=t[:].rearrange("p (j f) -> p j f", f=NBRS * D), in_=nb_v[:, j0 : j0 + cnt, :]
+            )
+            for i in range(cnt):
+                for n in range(NBRS):
+                    src[(j0 + i, n + 1)] = (t[:].bitcast(F32), (i * NBRS + n) * WORDS)
+
+        load_neighbors()
+
+        w_raw = const.tile([P, 4 * L], BF16, name="w_raw")
+        nc.sync.dma_start(out=w_raw[:].rearrange("q (u f) -> q u f", u=2), in_=w_v)
+        a_sb = const.tile([P, TILES * MEMBERS], BF16, name="a_sb")
+        nc.sync.dma_start(out=a_sb[:], in_=a_v)
+
+        for c in range(1, NB_BUFS):
+            load_neighbors()
+
+        w_grp = const.tile([P, L * 4], BF16, name="w_grp", align_bytes=64)
+        nc.vector.tensor_copy(
+            out=w_grp[:].rearrange("q (c t) -> q c t", t=4),
+            in_=w_raw[:].rearrange("q (t c) -> q c t", t=4),
+        )
+        w_codes = const.tile([P, L], U32, name="w_codes", align_bytes=64)
+        w_scales = const.tile([P, L], U8, name="w_scales", align_bytes=64)
+
+        deg = const.tile([P, TILES], F32, name="deg")
+        nc.vector.tensor_reduce(
+            out=deg[:],
+            in_=a_sb[:].rearrange("p (j k) -> p j k", k=MEMBERS),
+            axis=mybir.AxisListType.X,
+            op=ALU.add,
+        )
+        nc.vector.quantize_mx(out=w_codes[:].bitcast(FP8X4), scales=w_scales[:], in_=w_grp[:])
+        big = const.tile([P, TILES], F32, name="big")
+        nc.vector.tensor_single_scalar(out=big[:], in_=deg[:], scalar=0.5, op=ALU.is_gt)
+        kept = const.tile([P, TILES], F32, name="kept")
+        nc.vector.tensor_tensor(out=kept[:], in0=deg[:], in1=big[:], op=ALU.mult)
+        small = const.tile([P, TILES], F32, name="small")
+        nc.vector.tensor_scalar(
+            out=small[:], in0=big[:], scalar1=-1.0, scalar2=1.0, op0=ALU.mult, op1=ALU.add
+        )
+        factor = const.tile([P, TILES], F32, name="factor")
+        nc.vector.tensor_tensor(out=factor[:], in0=kept[:], in1=small[:], op=ALU.add)
+        recip = const.tile([P, TILES], F32, name="recip")
+        nc.vector.reciprocal(out=recip[:], in_=factor[:])
+
+        quantised = {}
+        stores = {}
+
+        def transpose_and_quantise(j):
+            g = grp.tile([P, MEMBERS * P * 4], BF16, name="g", align_bytes=64)
+            g32 = g[:].bitcast(F32)
+            for b in range(MEMBERS // 2):
+                xt = pst.tile([P, 4 * P], F32, name="xt")
+                for mm in range(2):
+                    view, w0 = src[(j, 2 * b + mm)]
+                    for u in range(2):
+                        nc.tensor.transpose(
+                            xt[:, (2 * mm + u) * P : (2 * mm + u + 1) * P],
+                            view[:, w0 + u * P : w0 + (u + 1) * P],
+                            ident[:],
+                        )
+                dst = g32[:, b * 4 * P : (b + 1) * 4 * P].rearrange("p (m r u) -> p m r u", m=2, u=2)
+                bank = xt[:].rearrange("p (m u r) -> p m r u", m=2, u=2)
+                if b in VECTOR_BANKS:
+                    nc.vector.tensor_copy(out=dst, in_=bank)
+                else:
+                    nc.scalar.copy(out=dst, in_=bank)
+            codes = qp.tile([P, MEMBERS * P], U32, name="codes", align_bytes=64)
+            scales = qp.tile([P, MEMBERS * P], U8, name="scales", align_bytes=64)
+            half = MEMBERS * P // 2
+            for h in range(2):
+                nc.vector.quantize_mx(
+                    out=codes[:, h * half : (h + 1) * half].bitcast(FP8X4),
+                    scales=scales[:, h * half : (h + 1) * half],
+                    in_=g[:, h * half * 4 : (h + 1) * half * 4],
+                )
+            quantised[j] = (codes, scales)
+
+        def multiply_and_store(j):
+            codes, scales = quantised[j]
+            acc = psa.tile([P, L], F32, name="acc")
+            for m in range(MEMBERS):
+                nc.tensor.matmul_mx(
+                    out=acc[:],
+                    lhsT=codes[:, m * P : (m + 1) * P].bitcast(FP8X4),
+                    lhsT_scale=scales[:, m * P : (m + 1) * P],
+                    rhs=w_codes[:].bitcast(FP8X4),
+                    rhs_scale=w_scales[:],
+                    start=(m == 0),
+                    stop=(m == MEMBERS - 1),
+                )
+            for j0, cnt in ST_CHUNKS:
+                if j0 <= j < j0 + cnt:
+                    if j == j0:
+                        stores[j0] = stp.tile([P, cnt * L], F32, name="res")
+                    res = stores[j0]
+                    nc.scalar.activation(
+                        out=res[:, (j - j0) * L : (j - j0 + 1) * L],
+                        in_=acc[:],
+                        func=ACT.Relu,
+                        scale=recip[:, j : j + 1],
+                    )
+                    if j == j0 + cnt - 1:
+                        nc.scalar.dma_start(
+                            out=out_v[:, j0 : j0 + cnt, :],
+                            in_=res[:].rearrange("p (j l) -> p j l", l=L),
+                        )
+
+        starts = [sum(RUNS[:s]) for s in range(len(RUNS))]
+        for s in range(len(RUNS) + 1):
+            if s < len(RUNS):
+                for j in range(starts[s], starts[s] + RUNS[s]):
+                    transpose_and_quantise(j)
+                    while state["nb"] < len(NB_CHUNKS):
+                        j0, cnt = NB_CHUNKS[state["nb"] - NB_BUFS]
+                        if j0 + cnt - 1 > j:
+                            break
+                        load_neighbors()
+            if s >= 1:
+                for j in range(starts[s - 1], starts[s - 1] + RUNS[s - 1]):
+                    multiply_and_store(j)

@@ -22,7 +22,7 @@ WORDS = D // 2
 
 FLOPS = 2 * NODES * MEMBERS * D * L
 
-RUNS = [1, 1] + [2] * 14 + [1, 1]
+RUNS = [1] * 32
 NB_CHUNKS = [(0, 1), (1, 1)] + [(j, 2) for j in range(2, 30, 2)] + [(30, 1), (31, 1)]
 TG_CHUNKS = [(0, 1), (1, 3), (4, 4), (8, 8), (16, 8), (24, 8)]
 ST_CHUNKS = [(j, 4) for j in range(0, 28, 4)] + [(28, 2), (30, 1), (31, 1)]

@@ -27,7 +27,7 @@ NB_CHUNKS = [(0, 1), (1, 1)] + [(j, 2) for j in range(2, 30, 2)] + [(30, 1), (31
 TG_CHUNKS = [(0, 1), (1, 3), (4, 4), (8, 8), (16, 8), (24, 8)]
 ST_CHUNKS = [(j, 4) for j in range(0, 28, 4)] + [(28, 2), (30, 1), (31, 1)]
 NB_BUFS = 6
-VECTOR_BANKS = (3,)
+VECTOR_BANKS = ((3,), (1, 3))
 
 
 def tile_singlegcnlayer_t_kernel(tc, targets, neighbors, a, kernel, out):
@@ -136,7 +136,7 @@ def tile_singlegcnlayer_t_kernel(tc, targets, neighbors, a, kernel, out):
                         )
                 dst = g32[:, b * 4 * P : (b + 1) * 4 * P].rearrange("p (m r u) -> p m r u", m=2, u=2)
                 bank = xt[:].rearrange("p (m u r) -> p m r u", m=2, u=2)
-                if b in VECTOR_BANKS:
+                if b in VECTOR_BANKS[j % 2]:
                     nc.vector.tensor_copy(out=dst, in_=bank)
                 else:
                     nc.scalar.copy(out=dst, in_=bank)

@@ -22,12 +22,15 @@ WORDS = D // 2
 
 FLOPS = 2 * NODES * MEMBERS * D * L
 
-RUNS = [1] * 32
-NB_CHUNKS = [(0, 1), (1, 1)] + [(j, 2) for j in range(2, 30, 2)] + [(30, 1), (31, 1)]
-TG_CHUNKS = [(0, 1), (1, 3), (4, 4), (8, 8), (16, 8), (24, 8)]
+RUNS = [1] * 30 + [2]
+FIRST_PIECES = [(0, 1), (1, 2), (3, 2), (5, 2)]
+NB_CHUNKS = [(j, 1) for j in range(1, 8)] + [(j, 2) for j in range(8, 30, 2)] + [(30, 1), (31, 1)]
+TG_CHUNKS = [(0, 1), (1, 1), (2, 2), (4, 4), (8, 8), (16, 8), (24, 8)]
 ST_CHUNKS = [(j, 4) for j in range(0, 28, 4)] + [(28, 2), (30, 1), (31, 1)]
 NB_BUFS = 6
 VECTOR_BANKS = ((3,), (1, 3))
+WARM_FIRST = 8
+WARM_SECOND = 4
 
 
 def tile_singlegcnlayer_t_kernel(tc, targets, neighbors, a, kernel, out):
@@ -48,10 +51,19 @@ def tile_singlegcnlayer_t_kernel(tc, targets, neighbors, a, kernel, out):
         psa = ctx.enter_context(tc.psum_pool(name="psa", bufs=2))
         ctx.enter_context(tc.manual_schedule())
 
+        zeros = const.tile([P, 4 * P], BF16, name="zeros")
+        nc.vector.memset(zeros[:], 0.0)
         ident = const.tile([P, P], F32, name="ident")
         make_identity(nc, ident[:])
         warm = const.tile([P, 1], F32, name="warm")
         nc.scalar.activation(out=warm[:], in_=ident[:, 0:1], func=ACT.Relu)
+
+        def keep_clock_up(count):
+            idle = pst.tile([P, 4 * P], F32, name="xt")
+            for i in range(count):
+                nc.tensor.matmul(out=idle[:], lhsT=zeros[:, 0:P], rhs=zeros[:], start=True, stop=True)
+
+        keep_clock_up(WARM_FIRST)
 
         src = {}
         state = {"nb": 0, "tg": 0}
@@ -79,23 +91,18 @@ def tile_singlegcnlayer_t_kernel(tc, targets, neighbors, a, kernel, out):
                 for n in range(NBRS):
                     src[(j0 + i, n + 1)] = (t[:].bitcast(F32), (i * NBRS + n) * WORDS)
 
-        load_neighbors()
-
-        w_raw = const.tile([P, 4 * L], BF16, name="w_raw")
-        nc.sync.dma_start(out=w_raw[:].rearrange("q (u f) -> q u f", u=2), in_=w_v)
+        load_targets()
         a_sb = const.tile([P, TILES * MEMBERS], BF16, name="a_sb")
         nc.sync.dma_start(out=a_sb[:], in_=a_v)
-
-        for c in range(1, NB_BUFS):
+        for n0, cnt in FIRST_PIECES:
+            t = const.tile([P, cnt * D], BF16, name="first%d" % n0)
+            nc.sync.dma_start(out=t[:], in_=nb_v[:, 0, n0 * D : (n0 + cnt) * D])
+            for i in range(cnt):
+                src[(0, n0 + i + 1)] = (t[:].bitcast(F32), i * WORDS)
+        w_raw = const.tile([P, 4 * L], BF16, name="w_raw")
+        nc.sync.dma_start(out=w_raw[:].rearrange("q (u f) -> q u f", u=2), in_=w_v)
+        for c in range(NB_BUFS):
             load_neighbors()
-
-        w_grp = const.tile([P, L * 4], BF16, name="w_grp", align_bytes=64)
-        nc.vector.tensor_copy(
-            out=w_grp[:].rearrange("q (c t) -> q c t", t=4),
-            in_=w_raw[:].rearrange("q (t c) -> q c t", t=4),
-        )
-        w_codes = const.tile([P, L], U32, name="w_codes", align_bytes=64)
-        w_scales = const.tile([P, L], U8, name="w_scales", align_bytes=64)
 
         deg = const.tile([P, TILES], F32, name="deg")
         nc.vector.tensor_reduce(
@@ -104,7 +111,6 @@ def tile_singlegcnlayer_t_kernel(tc, targets, neighbors, a, kernel, out):
             axis=mybir.AxisListType.X,
             op=ALU.add,
         )
-        nc.vector.quantize_mx(out=w_codes[:].bitcast(FP8X4), scales=w_scales[:], in_=w_grp[:])
         big = const.tile([P, TILES], F32, name="big")
         nc.vector.tensor_single_scalar(out=big[:], in_=deg[:], scalar=0.5, op=ALU.is_gt)
         kept = const.tile([P, TILES], F32, name="kept")
@@ -118,10 +124,15 @@ def tile_singlegcnlayer_t_kernel(tc, targets, neighbors, a, kernel, out):
         recip = const.tile([P, TILES], F32, name="recip")
         nc.vector.reciprocal(out=recip[:], in_=factor[:])
 
+        w_grp = const.tile([P, L * 4], BF16, name="w_grp", align_bytes=64)
+        w_codes = const.tile([P, L], U32, name="w_codes", align_bytes=64)
+        w_scales = const.tile([P, L], U8, name="w_scales", align_bytes=64)
+
+        grouped = {}
         quantised = {}
         stores = {}
 
-        def transpose_and_quantise(j):
+        def transposes(j):
             g = grp.tile([P, MEMBERS * P * 4], BF16, name="g", align_bytes=64)
             g32 = g[:].bitcast(F32)
             for b in range(MEMBERS // 2):
@@ -140,6 +151,10 @@ def tile_singlegcnlayer_t_kernel(tc, targets, neighbors, a, kernel, out):
                     nc.vector.tensor_copy(out=dst, in_=bank)
                 else:
                     nc.scalar.copy(out=dst, in_=bank)
+            grouped[j] = g
+
+        def quantise(j):
+            g = grouped[j]
             codes = qp.tile([P, MEMBERS * P], U32, name="codes", align_bytes=64)
             scales = qp.tile([P, MEMBERS * P], U8, name="scales", align_bytes=64)
             half = MEMBERS * P // 2
@@ -185,7 +200,18 @@ def tile_singlegcnlayer_t_kernel(tc, targets, neighbors, a, kernel, out):
         for s in range(len(RUNS) + 1):
             if s < len(RUNS):
                 for j in range(starts[s], starts[s] + RUNS[s]):
-                    transpose_and_quantise(j)
+                    transposes(j)
+                    if j == 0:
+                        keep_clock_up(WARM_SECOND)
+                        nc.vector.tensor_copy(
+                            out=w_grp[:].rearrange("q (c t) -> q c t", t=4),
+                            in_=w_raw[:].rearrange("q (t c) -> q c t", t=4),
+                        )
+                    quantise(j)
+                    if j == 0:
+                        nc.vector.quantize_mx(
+                            out=w_codes[:].bitcast(FP8X4), scales=w_scales[:], in_=w_grp[:]
+                        )
                     while state["nb"] < len(NB_CHUNKS):
                         j0, cnt = NB_CHUNKS[state["nb"] - NB_BUFS]
                         if j0 + cnt - 1 > j:

from contextlib import ExitStack

import concourse.mybir as mybir
from concourse.masks import make_identity

F32 = mybir.dt.float32
BF16 = mybir.dt.bfloat16
U32 = mybir.dt.uint32
U8 = mybir.dt.uint8
FP8X4 = mybir.dt.float8_e4m3fn_x4
ALU = mybir.AluOpType
ACT = mybir.ActivationFunctionType

P = 128
NODES = 4096
TILES = NODES // P
NBRS = 7
MEMBERS = NBRS + 1
D = 512
L = 256
WORDS = D // 2

FLOPS = 2 * NODES * MEMBERS * D * L

RUNS = [1] * 30 + [2]
FIRST_PIECES = [(0, 1), (1, 2), (3, 2), (5, 2)]
NB_CHUNKS = [(j, 1) for j in range(1, 8)] + [(j, 2) for j in range(8, 30, 2)] + [(30, 1), (31, 1)]
TG_CHUNKS = [(0, 1), (1, 1), (2, 2), (4, 4), (8, 8), (16, 8), (24, 8)]
ST_CHUNKS = [(j, 4) for j in range(0, 28, 4)] + [(28, 2), (30, 1), (31, 1)]
NB_BUFS = 6
VECTOR_BANKS = ((3,), (1, 3))
WARM_FIRST = 8
WARM_SECOND = 4


def tile_singlegcnlayer_t_kernel(tc, targets, neighbors, a, kernel, out):
    nc = tc.nc
    tg_v = targets.rearrange("b n d -> (b n) d").rearrange("(p j) d -> p j d", j=TILES)
    nb_v = neighbors.rearrange("b n k d -> (b n) (k d)").rearrange("(p j) f -> p j f", j=TILES)
    a_v = a.rearrange("b n k -> (b n) k").rearrange("(p j) k -> p (j k)", j=TILES)
    out_v = out.rearrange("b n l -> (b n) l").rearrange("(p j) l -> p j l", j=TILES)
    w_v = kernel.rearrange("(u q e) c -> q u (e c)", u=2, e=2)

    with ExitStack() as ctx:
        const = ctx.enter_context(tc.tile_pool(name="const", bufs=1))
        nbp = ctx.enter_context(tc.tile_pool(name="nbp", bufs=NB_BUFS))
        grp = ctx.enter_context(tc.tile_pool(name="grp", bufs=4))
        qp = ctx.enter_context(tc.tile_pool(name="qp", bufs=4))
        stp = ctx.enter_context(tc.tile_pool(name="stp", bufs=3))
        pst = ctx.enter_context(tc.psum_pool(name="pst", bufs=6))
        psa = ctx.enter_context(tc.psum_pool(name="psa", bufs=2))
        ctx.enter_context(tc.manual_schedule())

        zeros = const.tile([P, 4 * P], BF16, name="zeros")
        nc.vector.memset(zeros[:], 0.0)
        ident = const.tile([P, P], F32, name="ident")
        make_identity(nc, ident[:])
        warm = const.tile([P, 1], F32, name="warm")
        nc.scalar.activation(out=warm[:], in_=ident[:, 0:1], func=ACT.Relu)

        def keep_clock_up(count):
            idle = pst.tile([P, 4 * P], F32, name="xt")
            for i in range(count):
                nc.tensor.matmul(out=idle[:], lhsT=zeros[:, 0:P], rhs=zeros[:], start=True, stop=True)

        keep_clock_up(WARM_FIRST)

        src = {}
        state = {"nb": 0, "tg": 0}

        def load_targets():
            j0, cnt = TG_CHUNKS[state["tg"]]
            state["tg"] += 1
            t = const.tile([P, cnt * D], BF16, name="tg%d" % j0)
            nc.sync.dma_start(
                out=t[:].rearrange("p (j d) -> p j d", d=D), in_=tg_v[:, j0 : j0 + cnt, :]
            )
            for i in range(cnt):
                src[(j0 + i, 0)] = (t[:].bitcast(F32), i * WORDS)

        def load_neighbors():
            j0, cnt = NB_CHUNKS[state["nb"]]
            state["nb"] += 1
            while state["tg"] < len(TG_CHUNKS) and TG_CHUNKS[state["tg"]][0] <= j0:
                load_targets()
            t = nbp.tile([P, cnt * NBRS * D], BF16, name="nb")
            nc.sync.dma_start(
                out=t[:].rearrange("p (j f) -> p j f", f=NBRS * D), in_=nb_v[:, j0 : j0 + cnt, :]
            )
            for i in range(cnt):
                for n in range(NBRS):
                    src[(j0 + i, n + 1)] = (t[:].bitcast(F32), (i * NBRS + n) * WORDS)

        load_targets()
        a_sb = const.tile([P, TILES * MEMBERS], BF16, name="a_sb")
        nc.sync.dma_start(out=a_sb[:], in_=a_v)
        for n0, cnt in FIRST_PIECES:
            t = const.tile([P, cnt * D], BF16, name="first%d" % n0)
            nc.sync.dma_start(out=t[:], in_=nb_v[:, 0, n0 * D : (n0 + cnt) * D])
            for i in range(cnt):
                src[(0, n0 + i + 1)] = (t[:].bitcast(F32), i * WORDS)
        w_raw = const.tile([P, 4 * L], BF16, name="w_raw")
        nc.sync.dma_start(out=w_raw[:].rearrange("q (u f) -> q u f", u=2), in_=w_v)
        for c in range(NB_BUFS):
            load_neighbors()

        deg = const.tile([P, TILES], F32, name="deg")
        nc.vector.tensor_reduce(
            out=deg[:],
            in_=a_sb[:].rearrange("p (j k) -> p j k", k=MEMBERS),
            axis=mybir.AxisListType.X,
            op=ALU.add,
        )
        big = const.tile([P, TILES], F32, name="big")
        nc.vector.tensor_single_scalar(out=big[:], in_=deg[:], scalar=0.5, op=ALU.is_gt)
        kept = const.tile([P, TILES], F32, name="kept")
        nc.vector.tensor_tensor(out=kept[:], in0=deg[:], in1=big[:], op=ALU.mult)
        small = const.tile([P, TILES], F32, name="small")
        nc.vector.tensor_scalar(
            out=small[:], in0=big[:], scalar1=-1.0, scalar2=1.0, op0=ALU.mult, op1=ALU.add
        )
        factor = const.tile([P, TILES], F32, name="factor")
        nc.vector.tensor_tensor(out=factor[:], in0=kept[:], in1=small[:], op=ALU.add)
        recip = const.tile([P, TILES], F32, name="recip")
        nc.vector.reciprocal(out=recip[:], in_=factor[:])

        w_grp = const.tile([P, L * 4], BF16, name="w_grp", align_bytes=64)
        w_codes = const.tile([P, L], U32, name="w_codes", align_bytes=64)
        w_scales = const.tile([P, L], U8, name="w_scales", align_bytes=64)

        grouped = {}
        quantised = {}
        stores = {}

        def transposes(j):
            g = grp.tile([P, MEMBERS * P * 4], BF16, name="g", align_bytes=64)
            g32 = g[:].bitcast(F32)
            for b in range(MEMBERS // 2):
                xt = pst.tile([P, 4 * P], F32, name="xt")
                for mm in range(2):
                    view, w0 = src[(j, 2 * b + mm)]
                    for u in range(2):
                        nc.tensor.transpose(
                            xt[:, (2 * mm + u) * P : (2 * mm + u + 1) * P],
                            view[:, w0 + u * P : w0 + (u + 1) * P],
                            ident[:],
                        )
                dst = g32[:, b * 4 * P : (b + 1) * 4 * P].rearrange("p (m r u) -> p m r u", m=2, u=2)
                bank = xt[:].rearrange("p (m u r) -> p m r u", m=2, u=2)
                if b in VECTOR_BANKS[j % 2]:
                    nc.vector.tensor_copy(out=dst, in_=bank)
                else:
                    nc.scalar.copy(out=dst, in_=bank)
            grouped[j] = g

        def quantise(j):
            g = grouped[j]
            codes = qp.tile([P, MEMBERS * P], U32, name="codes", align_bytes=64)
            scales = qp.tile([P, MEMBERS * P], U8, name="scales", align_bytes=64)
            half = MEMBERS * P // 2
            for h in range(2):
                nc.vector.quantize_mx(
                    out=codes[:, h * half : (h + 1) * half].bitcast(FP8X4),
                    scales=scales[:, h * half : (h + 1) * half],
                    in_=g[:, h * half * 4 : (h + 1) * half * 4],
                )
            quantised[j] = (codes, scales)

        def multiply_and_store(j):
            codes, scales = quantised[j]
            acc = psa.tile([P, L], F32, name="acc")
            for m in range(MEMBERS):
                nc.tensor.matmul_mx(
                    out=acc[:],
                    lhsT=codes[:, m * P : (m + 1) * P].bitcast(FP8X4),
                    lhsT_scale=scales[:, m * P : (m + 1) * P],
                    rhs=w_codes[:].bitcast(FP8X4),
                    rhs_scale=w_scales[:],
                    start=(m == 0),
                    stop=(m == MEMBERS - 1),
                )
            for j0, cnt in ST_CHUNKS:
                if j0 <= j < j0 + cnt:
                    if j == j0:
                        stores[j0] = stp.tile([P, cnt * L], F32, name="res")
                    res = stores[j0]
                    nc.scalar.activation(
                        out=res[:, (j - j0) * L : (j - j0 + 1) * L],
                        in_=acc[:],
                        func=ACT.Relu,
                        scale=recip[:, j : j + 1],
                    )
                    if j == j0 + cnt - 1:
                        nc.scalar.dma_start(
                            out=out_v[:, j0 : j0 + cnt, :],
                            in_=res[:].rearrange("p (j l) -> p j l", l=L),
                        )

        starts = [sum(RUNS[:s]) for s in range(len(RUNS))]
        for s in range(len(RUNS) + 1):
            if s < len(RUNS):
                for j in range(starts[s], starts[s] + RUNS[s]):
                    transposes(j)
                    if j == 0:
                        keep_clock_up(WARM_SECOND)
                        nc.vector.tensor_copy(
                            out=w_grp[:].rearrange("q (c t) -> q c t", t=4),
                            in_=w_raw[:].rearrange("q (t c) -> q c t", t=4),
                        )
                    quantise(j)
                    if j == 0:
                        nc.vector.quantize_mx(
                            out=w_codes[:].bitcast(FP8X4), scales=w_scales[:], in_=w_grp[:]
                        )
                    while state["nb"] < len(NB_CHUNKS):
                        j0, cnt = NB_CHUNKS[state["nb"] - NB_BUFS]
                        if j0 + cnt - 1 > j:
                            break
                        load_neighbors()
            if s >= 1:
                for j in range(starts[s - 1], starts[s - 1] + RUNS[s - 1]):
                    multiply_and_store(j)
